import numpy as np
import ml_dtypes


def mxq(x, axis, fmt="e4m3"):
    dtype, down = {"e4m3": (ml_dtypes.float8_e4m3fn, 7), "e5m2": (ml_dtypes.float8_e5m2, 14)}[fmt]
    v = np.moveaxis(np.asarray(x, np.float32).astype(ml_dtypes.bfloat16).astype(np.float64), axis, -1)
    blocks = v.reshape(v.shape[:-1] + (-1, 32))
    amax = np.abs(blocks).max(-1, keepdims=True)
    byte = np.maximum(np.where(amax > 0, np.frexp(amax)[1] - 1 + 127, 0) - down, 1)
    scale = np.exp2(byte - 127.0)
    codes = (blocks / scale).astype(np.float32).astype(dtype).astype(np.float64)
    return np.moveaxis((codes * scale).reshape(v.shape), -1, axis)


WIDE = False


def mx_kscale(k):
    if not WIDE:
        return np.ones(k)
    levels = np.array([20, -20, 10, -10, 0])
    a = np.random.permutation(np.resize(levels, k // 512 * 4)).reshape(k // 512, 4)
    idx = np.arange(k)
    return np.exp2(a[idx // 512, idx % 128 // 32])


BF16 = ml_dtypes.bfloat16


def bf(x):
    return np.asarray(x, np.float32).astype(BF16)


def f64(x):
    return np.asarray(x).astype(np.float64)


B, S, H, O = 2, 512, 1024, 4608
T = B * S


def setup_inputs():
    s = mx_kscale(T).reshape(B, S, 1)
    x = np.random.standard_normal((B, S, H)) * s
    w_quantized = np.random.standard_normal((O, H)) * 0.03
    smooth_scale = np.random.uniform(0.5, 2.0, H)
    bias = np.random.standard_normal(O) * 0.3
    g = np.random.standard_normal((B, S, O)) * np.exp2(np.random.randint(-12, 1, (B, S, 1))) / s
    return {"x": bf(x), "w_quantized": bf(w_quantized), "smooth_scale": bf(smooth_scale),
            "bias": bf(bias), "grad_out": bf(g)}


def reference(x, w_quantized, smooth_scale, bias, grad_out):
    x_s = (f64(x) * f64(smooth_scale)).reshape(T, H)
    g = f64(grad_out).reshape(T, O)
    return mxq(g, 0, "e5m2").T @ mxq(x_s, 0, "e4m3")

@@ -1,0 +1,187 @@
+from contextlib import ExitStack
+
+import concourse.mybir as mybir
+
+BF16 = mybir.dt.bfloat16
+F32 = mybir.dt.float32
+U32 = mybir.dt.uint32
+U8 = mybir.dt.uint8
+E4M3 = mybir.dt.float8_e4m3fn_x4
+E5M2 = mybir.dt.float8_e5m2_x4
+
+P = 128
+PACK = 4
+K_PASS = P * PACK
+T, H, O = 1024, 1024, 4608
+PASSES = T // K_PASS
+N_TILE = 512
+HALVES = H // N_TILE
+ROWS = 4
+GROUP = P * ROWS
+GROUPS = O // GROUP
+CHUNKS = [1,2,3,3]
+VECTOR_UNITS = [5]
+
+FLOPS = 2 * T * H * O
+BYTES = 2 * T * H + 2 * H + 2 * T * O + 4 * O * H
+
+
+def tile_fp4ditlinear_kernel(tc, x, w_quantized, smooth_scale, bias, grad_out, out):
+    nc = tc.nc
+    xf = x.flatten_outer_dims()
+    gf = grad_out.flatten_outer_dims()
+    with ExitStack() as ctx:
+        keep = ctx.enter_context(tc.tile_pool(name="keep", bufs=1))
+        stage = ctx.enter_context(tc.tile_pool(name="stage", bufs=4))
+        quant = ctx.enter_context(tc.tile_pool(name="quant", bufs=3))
+        outs = ctx.enter_context(tc.tile_pool(name="outs", bufs=5))
+        spsum = ctx.enter_context(tc.psum_pool(name="spsum", bufs=1))
+        psum = ctx.enter_context(tc.psum_pool(name="psum", bufs=6))
+        ctx.enter_context(tc.manual_schedule())
+
+        srow = keep.tile([P, H], BF16, name="srow")
+        nc.vector.memset(srow[:], 0.0)
+        ones = keep.tile([P, P], BF16, name="ones")
+        nc.gpsimd.memset(ones[:], 1.0)
+        xraw = []
+        for c in range(PASSES):
+            xr = keep.tile([P, PACK, H], BF16, name="xraw%d" % c)
+            nc.sync.dma_start(out=xr[:], in_=xf[c * K_PASS:(c + 1) * K_PASS, :].rearrange("(p j) h -> p j h", j=PACK))
+            xraw.append(xr)
+            if c == 0:
+                nc.sync.dma_start(out=srow[0:1, :], in_=smooth_scale.unsqueeze(0))
+        where = []
+        graw = []
+        col = 0
+        for ch, n_groups in enumerate(CHUNKS):
+            width = n_groups * GROUP
+            pair = []
+            for c in range(PASSES):
+                gr = keep.tile([P, PACK, width], BF16, name="graw%d_%d" % (ch, c))
+                nc.sync.dma_start(
+                    out=gr[:],
+                    in_=gf[c * K_PASS:(c + 1) * K_PASS, col:col + width].rearrange("(p j) w -> p j w", j=PACK),
+                )
+                pair.append(gr)
+            graw.append(pair)
+            for i in range(n_groups):
+                where.append((ch, i * GROUP))
+            col += width
+
+        s_ps = []
+        for hh in range(HALVES):
+            sp = spsum.tile([P, N_TILE], F32, name="s_ps%d" % hh)
+            nc.tensor.matmul(out=sp[:], lhsT=ones[:], rhs=srow[:, hh * N_TILE:(hh + 1) * N_TILE], start=True, stop=True)
+            s_ps.append(sp)
+
+        x_codes = keep.tile([P, HALVES, PASSES, N_TILE], U32, name="x_codes", align_bytes=64)
+        x_scales = keep.tile([P, HALVES, PASSES, N_TILE], U8, name="x_scales", align_bytes=64)
+        xg = {}
+        gg = {}
+        g_codes = {}
+        g_scales = {}
+        ost = {}
+
+        def x_mult(c, hh):
+            if c == 0:
+                xg[hh] = stage.tile([P, PASSES, N_TILE, PACK], BF16, name="xg%d" % hh, tag="grouped", align_bytes=64)
+            nc.vector.tensor_tensor(
+                out=xg[hh][:, c],
+                in0=xraw[c][:, :, hh * N_TILE:(hh + 1) * N_TILE].rearrange("p j w -> p w j"),
+                in1=s_ps[hh][:].unsqueeze(2).to_broadcast([P, N_TILE, PACK]),
+                op=mybir.AluOpType.mult,
+            )
+
+        def x_quant(hh):
+            nc.vector.quantize_mx(
+                out=x_codes[:, hh].rearrange("p c w -> p (c w)").bitcast(E4M3),
+                scales=x_scales[:, hh].rearrange("p c w -> p (c w)"),
+                in_=xg[hh][:].rearrange("p c w j -> p (c w j)"),
+            )
+
+        def regroup(g, c, engine):
+            if g >= GROUPS:
+                return
+            if c == 0:
+                gg[g] = stage.tile([P, PASSES, GROUP * PACK], BF16, name="gg%d" % g, tag="grouped", align_bytes=64)
+            ch, off = where[g]
+            src = graw[ch][c][:, :, off:off + GROUP].rearrange("p j (m r) -> p m j r", r=ROWS)
+            dst = gg[g][:, c, :].rearrange("p (r m j) -> p m j r", r=ROWS, m=P, j=PACK)
+            if engine == "v":
+                nc.vector.tensor_copy(out=dst, in_=src)
+            else:
+                nc.scalar.copy(out=dst, in_=src)
+
+        def g_quant(g):
+            if g >= GROUPS:
+                return
+            g_codes[g] = quant.tile([P, PASSES, GROUP], U32, name="gc%d" % g, tag="codes", align_bytes=64)
+            g_scales[g] = quant.tile([P, PASSES, GROUP], U8, name="gs%d" % g, tag="scales", align_bytes=64)
+            nc.vector.quantize_mx(
+                out=g_codes[g][:].rearrange("p c w -> p (c w)").bitcast(E5M2),
+                scales=g_scales[g][:].rearrange("p c w -> p (c w)"),
+                in_=gg[g][:].rearrange("p c f -> p (c f)"),
+            )
+
+        def unit(g, r, n, engine):
+            acc = psum.tile([P, N_TILE], F32, name="acc", tag="acc")
+            for c in range(PASSES):
+                nc.tensor.matmul_mx(
+                    out=acc[:],
+                    lhsT=g_codes[g][:, c, r * P:(r + 1) * P].bitcast(E5M2),
+                    lhsT_scale=g_scales[g][:, c, r * P:(r + 1) * P],
+                    rhs=x_codes[:, n, c, :].bitcast(E4M3),
+                    rhs_scale=x_scales[:, n, c, :],
+                    start=(c == 0),
+                    stop=(c == PASSES - 1),
+                )
+            dst = ost[g][:, r, n * N_TILE:(n + 1) * N_TILE]
+            if engine == "v":
+                nc.vector.tensor_copy(out=dst, in_=acc[:])
+            else:
+                nc.scalar.copy(out=dst, in_=acc[:])
+
+        def new_out(g):
+            ost[g] = outs.tile([P, ROWS, H], F32, name="ost%d" % g, tag="ost")
+
+        def store(g, r=None):
+            rows = out[g * GROUP:(g + 1) * GROUP, :].rearrange("(q r) h -> q r h", r=ROWS)
+            if r is None:
+                nc.sync.dma_start(out=rows, in_=ost[g][:])
+            else:
+                nc.sync.dma_start(out=rows[:, r, :], in_=ost[g][:, r, :])
+
+        x_mult(0, 0)
+        x_mult(1, 0)
+        regroup(0, 0, "s")
+        x_quant(0)
+        regroup(0, 1, "v")
+        x_mult(0, 1)
+        g_quant(0)
+        regroup(1, 0, "s")
+        new_out(0)
+        for r in range(ROWS):
+            unit(0, r, 0, "s")
+        x_mult(1, 1)
+        regroup(1, 1, "s")
+        regroup(2, 0, "v")
+        x_quant(1)
+        for r in range(ROWS):
+            unit(0, r, 1, "s")
+        store(0)
+        g_quant(1)
+        regroup(2, 1, "v")
+
+        for g in range(1, GROUPS):
+            last = g == GROUPS - 1
+            new_out(g)
+            regroup(g + 2, 0, "v")
+            g_quant(g + 1)
+            for u in range(ROWS * HALVES):
+                if u == ROWS * HALVES // 2:
+                    regroup(g + 2, 1, "v")
+                unit(g, u // HALVES, u % HALVES, "v" if u in VECTOR_UNITS else "s")
+                if last and u % HALVES == HALVES - 1:
+                    store(g, u // HALVES)
+            if not last:
+                store(g)

@@ -19,7 +19,8 @@ HALVES = H // N_TILE
 ROWS = 4
 GROUP = P * ROWS
 GROUPS = O // GROUP
-CHUNKS = [1,2,3,3]
+CHUNKS = [1,3,5]
+PIECES = [1,1,1,1,2,2,2,2,4]
 VECTOR_UNITS = [5]
 
 FLOPS = 2 * T * H * O
@@ -35,44 +36,53 @@ def tile_fp4ditlinear_kernel(tc, x, w_quantized, smooth_scale, bias, grad_out, o
         stage = ctx.enter_context(tc.tile_pool(name="stage", bufs=4))
         quant = ctx.enter_context(tc.tile_pool(name="quant", bufs=3))
         outs = ctx.enter_context(tc.tile_pool(name="outs", bufs=5))
-        spsum = ctx.enter_context(tc.psum_pool(name="spsum", bufs=1))
-        psum = ctx.enter_context(tc.psum_pool(name="psum", bufs=6))
+        psum = ctx.enter_context(tc.psum_pool(name="psum", bufs=8))
         ctx.enter_context(tc.manual_schedule())
 
         srow = keep.tile([P, H], BF16, name="srow")
         nc.vector.memset(srow[:], 0.0)
         ones = keep.tile([P, P], BF16, name="ones")
         nc.gpsimd.memset(ones[:], 1.0)
-        xraw = []
-        for c in range(PASSES):
-            xr = keep.tile([P, PACK, H], BF16, name="xraw%d" % c)
-            nc.sync.dma_start(out=xr[:], in_=xf[c * K_PASS:(c + 1) * K_PASS, :].rearrange("(p j) h -> p j h", j=PACK))
-            xraw.append(xr)
-            if c == 0:
-                nc.sync.dma_start(out=srow[0:1, :], in_=smooth_scale.unsqueeze(0))
+
         where = []
-        graw = []
+        starts = []
         col = 0
         for ch, n_groups in enumerate(CHUNKS):
-            width = n_groups * GROUP
-            pair = []
-            for c in range(PASSES):
-                gr = keep.tile([P, PACK, width], BF16, name="graw%d_%d" % (ch, c))
-                nc.sync.dma_start(
-                    out=gr[:],
-                    in_=gf[c * K_PASS:(c + 1) * K_PASS, col:col + width].rearrange("(p j) w -> p j w", j=PACK),
-                )
-                pair.append(gr)
-            graw.append(pair)
+            starts.append(col)
             for i in range(n_groups):
                 where.append((ch, i * GROUP))
-            col += width
+            col += n_groups * GROUP
+        graw = [[None] * PASSES for ch in CHUNKS]
+        xraw = [None] * PASSES
 
-        s_ps = []
+        def load_g(ch, c):
+            width = CHUNKS[ch] * GROUP
+            gr = keep.tile([P, PACK, width], BF16, name="graw%d_%d" % (ch, c))
+            nc.sync.dma_start(
+                out=gr[:],
+                in_=gf[c * K_PASS:(c + 1) * K_PASS, starts[ch]:starts[ch] + width].rearrange("(p j) w -> p j w", j=PACK),
+            )
+            graw[ch][c] = gr
+
+        def load_x(c):
+            xr = keep.tile([P, PACK, H], BF16, name="xraw%d" % c)
+            nc.sync.dma_start(out=xr[:], in_=xf[c * K_PASS:(c + 1) * K_PASS, :].rearrange("(p j) h -> p j h", j=PACK))
+            xraw[c] = xr
+
+        load_g(0, 0)
+        nc.sync.dma_start(out=srow[0:1, :], in_=smooth_scale.unsqueeze(0))
+        load_g(0, 1)
+        load_x(0)
+        load_x(1)
+        for ch in range(1, len(CHUNKS)):
+            for c in range(PASSES):
+                load_g(ch, c)
+
+        s_sb = keep.tile([P, H], BF16, name="s_sb")
         for hh in range(HALVES):
-            sp = spsum.tile([P, N_TILE], F32, name="s_ps%d" % hh)
+            sp = psum.tile([P, N_TILE], F32, name="s_ps", tag="acc")
             nc.tensor.matmul(out=sp[:], lhsT=ones[:], rhs=srow[:, hh * N_TILE:(hh + 1) * N_TILE], start=True, stop=True)
-            s_ps.append(sp)
+            nc.scalar.copy(out=s_sb[:, hh * N_TILE:(hh + 1) * N_TILE], in_=sp[:])
 
         x_codes = keep.tile([P, HALVES, PASSES, N_TILE], U32, name="x_codes", align_bytes=64)
         x_scales = keep.tile([P, HALVES, PASSES, N_TILE], U8, name="x_scales", align_bytes=64)
@@ -82,14 +92,27 @@ def tile_fp4ditlinear_kernel(tc, x, w_quantized, smooth_scale, bias, grad_out, o
         g_scales = {}
         ost = {}
 
-        def x_mult(c, hh):
-            if c == 0:
-                xg[hh] = stage.tile([P, PASSES, N_TILE, PACK], BF16, name="xg%d" % hh, tag="grouped", align_bytes=64)
+        def copy_on(engine, dst, src):
+            if engine == "v":
+                nc.vector.tensor_copy(out=dst, in_=src)
+            else:
+                nc.scalar.copy(out=dst, in_=src)
+
+        def x_mult(c):
             nc.vector.tensor_tensor(
-                out=xg[hh][:, c],
-                in0=xraw[c][:, :, hh * N_TILE:(hh + 1) * N_TILE].rearrange("p j w -> p w j"),
-                in1=s_ps[hh][:].unsqueeze(2).to_broadcast([P, N_TILE, PACK]),
+                out=xraw[c][:],
+                in0=xraw[c][:],
+                in1=s_sb[:].unsqueeze(1).to_broadcast([P, PACK, H]),
                 op=mybir.AluOpType.mult,
+            )
+
+        def x_regroup(c, hh, engine):
+            if hh not in xg:
+                xg[hh] = stage.tile([P, PASSES, N_TILE, PACK], BF16, name="xg%d" % hh, tag="grouped", align_bytes=64)
+            copy_on(
+                engine,
+                xg[hh][:, c].rearrange("p (a i) j -> p a j i", i=4),
+                xraw[c][:, :, hh * N_TILE:(hh + 1) * N_TILE].rearrange("p j (a i) -> p a j i", i=4),
             )
 
         def x_quant(hh):
@@ -102,15 +125,14 @@ def tile_fp4ditlinear_kernel(tc, x, w_quantized, smooth_scale, bias, grad_out, o
         def regroup(g, c, engine):
             if g >= GROUPS:
                 return
-            if c == 0:
+            if g not in gg:
                 gg[g] = stage.tile([P, PASSES, GROUP * PACK], BF16, name="gg%d" % g, tag="grouped", align_bytes=64)
             ch, off = where[g]
-            src = graw[ch][c][:, :, off:off + GROUP].rearrange("p j (m r) -> p m j r", r=ROWS)
-            dst = gg[g][:, c, :].rearrange("p (r m j) -> p m j r", r=ROWS, m=P, j=PACK)
-            if engine == "v":
-                nc.vector.tensor_copy(out=dst, in_=src)
-            else:
-                nc.scalar.copy(out=dst, in_=src)
+            copy_on(
+                engine,
+                gg[g][:, c, :].rearrange("p (r m j) -> p m j r", r=ROWS, m=P, j=PACK),
+                graw[ch][c][:, :, off:off + GROUP].rearrange("p j (m r) -> p m j r", r=ROWS),
+            )
 
         def g_quant(g):
             if g >= GROUPS:
@@ -135,45 +157,41 @@ def tile_fp4ditlinear_kernel(tc, x, w_quantized, smooth_scale, bias, grad_out, o
                     start=(c == 0),
                     stop=(c == PASSES - 1),
                 )
-            dst = ost[g][:, r, n * N_TILE:(n + 1) * N_TILE]
-            if engine == "v":
-                nc.vector.tensor_copy(out=dst, in_=acc[:])
-            else:
-                nc.scalar.copy(out=dst, in_=acc[:])
+            copy_on(engine, ost[g][:, r, n * N_TILE:(n + 1) * N_TILE], acc[:])
 
         def new_out(g):
             ost[g] = outs.tile([P, ROWS, H], F32, name="ost%d" % g, tag="ost")
 
-        def store(g, r=None):
-            rows = out[g * GROUP:(g + 1) * GROUP, :].rearrange("(q r) h -> q r h", r=ROWS)
-            if r is None:
-                nc.sync.dma_start(out=rows, in_=ost[g][:])
-            else:
-                nc.sync.dma_start(out=rows[:, r, :], in_=ost[g][:, r, :])
+        def store_after(g, r):
+            step = ROWS // PIECES[g]
+            if (r + 1) % step == 0:
+                rows = out[g * GROUP:(g + 1) * GROUP, :].rearrange("(q r) h -> q r h", r=ROWS)
+                nc.sync.dma_start(out=rows[:, r + 1 - step:r + 1, :], in_=ost[g][:, r + 1 - step:r + 1, :])
 
-        x_mult(0, 0)
-        x_mult(1, 0)
-        regroup(0, 0, "s")
-        x_quant(0)
+        regroup(0, 0, "v")
         regroup(0, 1, "v")
-        x_mult(0, 1)
         g_quant(0)
-        regroup(1, 0, "s")
-        new_out(0)
-        for r in range(ROWS):
-            unit(0, r, 0, "s")
-        x_mult(1, 1)
-        regroup(1, 1, "s")
-        regroup(2, 0, "v")
+        x_mult(0)
+        x_regroup(0, 0, "s")
+        x_mult(1)
+        x_regroup(0, 1, "s")
+        x_regroup(1, 0, "v")
+        x_quant(0)
+        x_regroup(1, 1, "v")
         x_quant(1)
-        for r in range(ROWS):
-            unit(0, r, 1, "s")
-        store(0)
+        regroup(1, 0, "s")
+        regroup(1, 1, "v")
         g_quant(1)
+        new_out(0)
+        for n in range(HALVES):
+            for r in range(ROWS):
+                unit(0, r, n, "s")
+                if n == HALVES - 1:
+                    store_after(0, r)
+        regroup(2, 0, "v")
         regroup(2, 1, "v")
 
         for g in range(1, GROUPS):
-            last = g == GROUPS - 1
             new_out(g)
             regroup(g + 2, 0, "v")
             g_quant(g + 1)
@@ -181,7 +199,5 @@ def tile_fp4ditlinear_kernel(tc, x, w_quantized, smooth_scale, bias, grad_out, o
                 if u == ROWS * HALVES // 2:
                     regroup(g + 2, 1, "v")
                 unit(g, u // HALVES, u % HALVES, "v" if u in VECTOR_UNITS else "s")
-                if last and u % HALVES == HALVES - 1:
-                    store(g, u // HALVES)
-            if not last:
-                store(g)
+                if u % HALVES == HALVES - 1:
+                    store_after(g, u // HALVES)

@@ -20,7 +20,7 @@ ROWS = 4
 GROUP = P * ROWS
 GROUPS = O // GROUP
 CHUNKS = [1,3,5]
-PIECES = [1,1,1,1,2,2,2,2,4]
+PIECES = [1,1,1,1,1,1,1,1,4]
 VECTOR_UNITS = [5]
 
 FLOPS = 2 * T * H * O
@@ -70,8 +70,8 @@ def tile_fp4ditlinear_kernel(tc, x, w_quantized, smooth_scale, bias, grad_out, o
             xraw[c] = xr
 
         load_g(0, 0)
-        nc.sync.dma_start(out=srow[0:1, :], in_=smooth_scale.unsqueeze(0))
         load_g(0, 1)
+        nc.sync.dma_start(out=srow[0:1, :], in_=smooth_scale.unsqueeze(0))
         load_x(0)
         load_x(1)
         for ch in range(1, len(CHUNKS)):

@@ -37,7 +37,6 @@ def tile_fp4ditlinear_kernel(tc, x, w_quantized, smooth_scale, bias, grad_out, o
         quant = ctx.enter_context(tc.tile_pool(name="quant", bufs=3))
         outs = ctx.enter_context(tc.tile_pool(name="outs", bufs=5))
         psum = ctx.enter_context(tc.psum_pool(name="psum", bufs=8))
-        ctx.enter_context(tc.manual_schedule())
 
         srow = keep.tile([P, H], BF16, name="srow")
         nc.vector.memset(srow[:], 0.0)

@@ -37,6 +37,7 @@ def tile_fp4ditlinear_kernel(tc, x, w_quantized, smooth_scale, bias, grad_out, o
         quant = ctx.enter_context(tc.tile_pool(name="quant", bufs=3))
         outs = ctx.enter_context(tc.tile_pool(name="outs", bufs=5))
         psum = ctx.enter_context(tc.psum_pool(name="psum", bufs=8))
+        ctx.enter_context(tc.manual_schedule())
 
         srow = keep.tile([P, H], BF16, name="srow")
         nc.vector.memset(srow[:], 0.0)
@@ -129,8 +130,8 @@ def tile_fp4ditlinear_kernel(tc, x, w_quantized, smooth_scale, bias, grad_out, o
             ch, off = where[g]
             copy_on(
                 engine,
-                gg[g][:, c, :].rearrange("p (r m j) -> p m j r", r=ROWS, m=P, j=PACK),
-                graw[ch][c][:, :, off:off + GROUP].rearrange("p j (m r) -> p m j r", r=ROWS),
+                gg[g][:, c, :].rearrange("p (a i j) -> p a j i", i=4, j=PACK),
+                graw[ch][c][:, :, off:off + GROUP].rearrange("p j (a i) -> p a j i", i=4),
             )
 
         def g_quant(g):
@@ -164,7 +165,7 @@ def tile_fp4ditlinear_kernel(tc, x, w_quantized, smooth_scale, bias, grad_out, o
         def store_after(g, r):
             step = ROWS // PIECES[g]
             if (r + 1) % step == 0:
-                rows = out[g * GROUP:(g + 1) * GROUP, :].rearrange("(q r) h -> q r h", r=ROWS)
+                rows = out[g * GROUP:(g + 1) * GROUP, :].rearrange("(r q) h -> q r h", r=ROWS)
                 nc.sync.dma_start(out=rows[:, r + 1 - step:r + 1, :], in_=ost[g][:, r + 1 - step:r + 1, :])
 
         regroup(0, 0, "v")

from contextlib import ExitStack

import concourse.mybir as mybir

BF16 = mybir.dt.bfloat16
F32 = mybir.dt.float32
U32 = mybir.dt.uint32
U8 = mybir.dt.uint8
E4M3 = mybir.dt.float8_e4m3fn_x4
E5M2 = mybir.dt.float8_e5m2_x4

P = 128
PACK = 4
K_PASS = P * PACK
T, H, O = 1024, 1024, 4608
PASSES = T // K_PASS
N_TILE = 512
HALVES = H // N_TILE
ROWS = 4
GROUP = P * ROWS
GROUPS = O // GROUP
CHUNKS = [1,3,5]
PIECES = [1,1,1,1,1,1,1,1,4]
VECTOR_UNITS = [5]

FLOPS = 2 * T * H * O
BYTES = 2 * T * H + 2 * H + 2 * T * O + 4 * O * H


def tile_fp4ditlinear_kernel(tc, x, w_quantized, smooth_scale, bias, grad_out, out):
    nc = tc.nc
    xf = x.flatten_outer_dims()
    gf = grad_out.flatten_outer_dims()
    with ExitStack() as ctx:
        keep = ctx.enter_context(tc.tile_pool(name="keep", bufs=1))
        stage = ctx.enter_context(tc.tile_pool(name="stage", bufs=4))
        quant = ctx.enter_context(tc.tile_pool(name="quant", bufs=3))
        outs = ctx.enter_context(tc.tile_pool(name="outs", bufs=5))
        psum = ctx.enter_context(tc.psum_pool(name="psum", bufs=8))
        ctx.enter_context(tc.manual_schedule())

        srow = keep.tile([P, H], BF16, name="srow")
        nc.vector.memset(srow[:], 0.0)
        ones = keep.tile([P, P], BF16, name="ones")
        nc.gpsimd.memset(ones[:], 1.0)

        where = []
        starts = []
        col = 0
        for ch, n_groups in enumerate(CHUNKS):
            starts.append(col)
            for i in range(n_groups):
                where.append((ch, i * GROUP))
            col += n_groups * GROUP
        graw = [[None] * PASSES for ch in CHUNKS]
        xraw = [None] * PASSES

        def load_g(ch, c):
            width = CHUNKS[ch] * GROUP
            gr = keep.tile([P, PACK, width], BF16, name="graw%d_%d" % (ch, c))
            nc.sync.dma_start(
                out=gr[:],
                in_=gf[c * K_PASS:(c + 1) * K_PASS, starts[ch]:starts[ch] + width].rearrange("(p j) w -> p j w", j=PACK),
            )
            graw[ch][c] = gr

        def load_x(c):
            xr = keep.tile([P, PACK, H], BF16, name="xraw%d" % c)
            nc.sync.dma_start(out=xr[:], in_=xf[c * K_PASS:(c + 1) * K_PASS, :].rearrange("(p j) h -> p j h", j=PACK))
            xraw[c] = xr

        load_g(0, 0)
        load_g(0, 1)
        nc.sync.dma_start(out=srow[0:1, :], in_=smooth_scale.unsqueeze(0))
        load_x(0)
        load_x(1)
        for ch in range(1, len(CHUNKS)):
            for c in range(PASSES):
                load_g(ch, c)

        s_sb = keep.tile([P, H], BF16, name="s_sb")
        for hh in range(HALVES):
            sp = psum.tile([P, N_TILE], F32, name="s_ps", tag="acc")
            nc.tensor.matmul(out=sp[:], lhsT=ones[:], rhs=srow[:, hh * N_TILE:(hh + 1) * N_TILE], start=True, stop=True)
            nc.scalar.copy(out=s_sb[:, hh * N_TILE:(hh + 1) * N_TILE], in_=sp[:])

        x_codes = keep.tile([P, HALVES, PASSES, N_TILE], U32, name="x_codes", align_bytes=64)
        x_scales = keep.tile([P, HALVES, PASSES, N_TILE], U8, name="x_scales", align_bytes=64)
        xg = {}
        gg = {}
        g_codes = {}
        g_scales = {}
        ost = {}

        def copy_on(engine, dst, src):
            if engine == "v":
                nc.vector.tensor_copy(out=dst, in_=src)
            else:
                nc.scalar.copy(out=dst, in_=src)

        def x_mult(c):
            nc.vector.tensor_tensor(
                out=xraw[c][:],
                in0=xraw[c][:],
                in1=s_sb[:].unsqueeze(1).to_broadcast([P, PACK, H]),
                op=mybir.AluOpType.mult,
            )

        def x_regroup(c, hh, engine):
            if hh not in xg:
                xg[hh] = stage.tile([P, PASSES, N_TILE, PACK], BF16, name="xg%d" % hh, tag="grouped", align_bytes=64)
            copy_on(
                engine,
                xg[hh][:, c].rearrange("p (a i) j -> p a j i", i=4),
                xraw[c][:, :, hh * N_TILE:(hh + 1) * N_TILE].rearrange("p j (a i) -> p a j i", i=4),
            )

        def x_quant(hh):
            nc.vector.quantize_mx(
                out=x_codes[:, hh].rearrange("p c w -> p (c w)").bitcast(E4M3),
                scales=x_scales[:, hh].rearrange("p c w -> p (c w)"),
                in_=xg[hh][:].rearrange("p c w j -> p (c w j)"),
            )

        def regroup(g, c, engine):
            if g >= GROUPS:
                return
            if g not in gg:
                gg[g] = stage.tile([P, PASSES, GROUP * PACK], BF16, name="gg%d" % g, tag="grouped", align_bytes=64)
            ch, off = where[g]
            copy_on(
                engine,
                gg[g][:, c, :].rearrange("p (a i j) -> p a j i", i=4, j=PACK),
                graw[ch][c][:, :, off:off + GROUP].rearrange("p j (a i) -> p a j i", i=4),
            )

        def g_quant(g):
            if g >= GROUPS:
                return
            g_codes[g] = quant.tile([P, PASSES, GROUP], U32, name="gc%d" % g, tag="codes", align_bytes=64)
            g_scales[g] = quant.tile([P, PASSES, GROUP], U8, name="gs%d" % g, tag="scales", align_bytes=64)
            nc.vector.quantize_mx(
                out=g_codes[g][:].rearrange("p c w -> p (c w)").bitcast(E5M2),
                scales=g_scales[g][:].rearrange("p c w -> p (c w)"),
                in_=gg[g][:].rearrange("p c f -> p (c f)"),
            )

        def unit(g, r, n, engine):
            acc = psum.tile([P, N_TILE], F32, name="acc", tag="acc")
            for c in range(PASSES):
                nc.tensor.matmul_mx(
                    out=acc[:],
                    lhsT=g_codes[g][:, c, r * P:(r + 1) * P].bitcast(E5M2),
                    lhsT_scale=g_scales[g][:, c, r * P:(r + 1) * P],
                    rhs=x_codes[:, n, c, :].bitcast(E4M3),
                    rhs_scale=x_scales[:, n, c, :],
                    start=(c == 0),
                    stop=(c == PASSES - 1),
                )
            copy_on(engine, ost[g][:, r, n * N_TILE:(n + 1) * N_TILE], acc[:])

        def new_out(g):
            ost[g] = outs.tile([P, ROWS, H], F32, name="ost%d" % g, tag="ost")

        def store_after(g, r):
            step = ROWS // PIECES[g]
            if (r + 1) % step == 0:
                rows = out[g * GROUP:(g + 1) * GROUP, :].rearrange("(r q) h -> q r h", r=ROWS)
                nc.sync.dma_start(out=rows[:, r + 1 - step:r + 1, :], in_=ost[g][:, r + 1 - step:r + 1, :])

        regroup(0, 0, "v")
        regroup(0, 1, "v")
        g_quant(0)
        x_mult(0)
        x_regroup(0, 0, "s")
        x_mult(1)
        x_regroup(0, 1, "s")
        x_regroup(1, 0, "v")
        x_quant(0)
        x_regroup(1, 1, "v")
        x_quant(1)
        regroup(1, 0, "s")
        regroup(1, 1, "v")
        g_quant(1)
        new_out(0)
        for n in range(HALVES):
            for r in range(ROWS):
                unit(0, r, n, "s")
                if n == HALVES - 1:
                    store_after(0, r)
        regroup(2, 0, "v")
        regroup(2, 1, "v")

        for g in range(1, GROUPS):
            new_out(g)
            regroup(g + 2, 0, "v")
            g_quant(g + 1)
            for u in range(ROWS * HALVES):
                if u == ROWS * HALVES // 2:
                    regroup(g + 2, 1, "v")
                unit(g, u // HALVES, u % HALVES, "v" if u in VECTOR_UNITS else "s")
                if u % HALVES == HALVES - 1:
                    store_after(g, u // HALVES)
